import numpy as np
import ml_dtypes


def mxq(x, axis, fmt="e4m3"):
    dtype, down = {"e4m3": (ml_dtypes.float8_e4m3fn, 7), "e5m2": (ml_dtypes.float8_e5m2, 14)}[fmt]
    v = np.moveaxis(np.asarray(x, np.float32).astype(ml_dtypes.bfloat16).astype(np.float64), axis, -1)
    blocks = v.reshape(v.shape[:-1] + (-1, 32))
    amax = np.abs(blocks).max(-1, keepdims=True)
    byte = np.maximum(np.where(amax > 0, np.frexp(amax)[1] - 1 + 127, 0) - down, 1)
    scale = np.exp2(byte - 127.0)
    codes = (blocks / scale).astype(np.float32).astype(dtype).astype(np.float64)
    return np.moveaxis((codes * scale).reshape(v.shape), -1, axis)


WIDE = False


def mx_kscale(k):
    if not WIDE:
        return np.ones(k)
    levels = np.array([10, -10, 5, -5, 0])
    a = np.random.permutation(np.resize(levels, k // 512 * 4)).reshape(k // 512, 4)
    idx = np.arange(k)
    return np.exp2(a[idx // 512, idx % 128 // 32])


BF16 = ml_dtypes.bfloat16


def bf(x):
    return np.asarray(x, np.float32).astype(BF16)


def f64(x):
    return np.asarray(x).astype(np.float64)


T, B, D, H, HD, A = 2048, 2, 1024, 1, 128, 128
HH = H * HD
HA = H * A
N = HH + HH + HA + HA
EPS = 1e-5
QK = 1.5


def layer_norm(x, w, b):
    mu = x.mean(-1, keepdims=True)
    var = np.square(x - mu).mean(-1, keepdims=True)
    return (x - mu) * (1.0 / np.sqrt(var + EPS)) * w + b


def setup_inputs():
    s = mx_kscale(D)
    col = np.concatenate([np.ones(HH + HH), QK * np.ones(HA + HA)])
    return {"src": bf(np.random.standard_normal((T, B, D))),
            "ln1_w": bf((1.0 + 0.1 * np.random.standard_normal(D)) * s),
            "ln1_b": bf(0.1 * np.random.standard_normal(D) * s),
            "w_uvqk": bf(np.random.standard_normal((D, N)) * col / np.sqrt(D) / s[:, None]),
            "b_uvqk": bf(0.1 * np.random.standard_normal(N))}


def reference(src, ln1_w, ln1_b, w_uvqk, b_uvqk):
    src_norm = layer_norm(f64(src), f64(ln1_w), f64(ln1_b))
    return (mxq(src_norm, 2, "e4m3") @ mxq(f64(w_uvqk), 0, "e4m3")) + f64(b_uvqk)

@@ -1,0 +1,211 @@
+import concourse.mybir as mybir
+from concourse.masks import make_identity
+
+F32 = mybir.dt.float32
+BF16 = mybir.dt.bfloat16
+U32 = mybir.dt.uint32
+U8 = mybir.dt.uint8
+FP8X4 = mybir.dt.float8_e4m3fn_x4
+ALU = mybir.AluOpType
+ACT = mybir.ActivationFunctionType
+
+P = 128
+ROWS = 2048 * 2
+D = 1024
+N = 512
+EPS = 1e-5
+PACK = 4
+K_PASS = P * PACK
+PASSES = D // K_PASS
+CHUNKS = D // P
+BN_WIDTH = 512
+BN_PARTS = D // BN_WIDTH
+UNIT_TILES = 2
+UNIT_COLS = UNIT_TILES * P
+UNITS = ROWS // UNIT_COLS
+BANK_F32 = 512
+BANK_CHUNKS = BANK_F32 // UNIT_COLS
+
+FLOPS = 2 * ROWS * D * N
+
+
+def side_by_side(copy, grouped, planes):
+    copy(
+        out=grouped.rearrange("p (c i) t -> p c t i", i=4),
+        in_=planes.rearrange("p t (c i) -> p c t i", i=4),
+    )
+
+
+def tile_stulayer_pa_t_kernel(tc, src, ln1_w, ln1_b, w_uvqk, b_uvqk, out):
+    nc = tc.nc
+    src_units = src.flatten_outer_dims().rearrange("(u p j) d -> u p j d", p=P, j=UNIT_TILES)
+    out_units = out.flatten_outer_dims().rearrange("(u p j) n -> u p j n", p=P, j=UNIT_TILES)
+
+    with (
+        tc.tile_pool(name="keep", bufs=1) as keep,
+        tc.tile_pool(name="stat", bufs=4) as stat,
+        tc.tile_pool(name="work", bufs=3) as work,
+        tc.psum_pool(name="turned", bufs=4) as turned_pool,
+        tc.psum_pool(name="sums", bufs=4) as sums_pool,
+    ):
+        x = []
+        for u in range(UNITS):
+            x.append(keep.tile([P, UNIT_TILES, D], BF16, name="x%d" % u))
+        w_planes = keep.tile([P, PASSES, PACK, N], BF16)
+        nc.sync.dma_start(out=x[0][:], in_=src_units[0])
+        nc.sync.dma_start(
+            out=w_planes[:], in_=w_uvqk.rearrange("(g t p) n -> p g t n", t=PACK, p=P)
+        )
+        for u in range(1, UNITS):
+            nc.sync.dma_start(out=x[u][:], in_=src_units[u])
+
+        vec_rows = keep.tile([P, P], BF16)
+        nc.vector.memset(vec_rows[:], 0.0)
+        nc.scalar.dma_start(out=vec_rows[0:CHUNKS, :], in_=ln1_w.rearrange("(c p) -> c p", p=P))
+        nc.scalar.dma_start(
+            out=vec_rows[CHUNKS : 2 * CHUNKS, :], in_=ln1_b.rearrange("(c p) -> c p", p=P)
+        )
+        bias = keep.tile([P, N], BF16)
+        nc.scalar.dma_start(out=bias[:], in_=b_uvqk.partition_broadcast(P))
+
+        ident = keep.tile([P, P], F32)
+        make_identity(nc, ident[:])
+        minus_half = keep.tile([P, UNIT_TILES], F32)
+        nc.vector.memset(minus_half[:], -0.5)
+
+        vec_f32 = keep.tile([P, P], F32)
+        nc.vector.tensor_copy(out=vec_f32[:], in_=vec_rows[:])
+        vec_turned = turned_pool.tile([P, BANK_CHUNKS, UNIT_COLS], F32, tag="turned")
+        nc.tensor.transpose(vec_turned[:, 0, 0:P], vec_f32[:], ident[:])
+        gain_shift = keep.tile([P, 2 * CHUNKS], F32)
+        nc.vector.tensor_copy(out=gain_shift[:], in_=vec_turned[:, 0, 0 : 2 * CHUNKS])
+
+        w_grouped = keep.tile([P, PASSES, N, PACK], BF16, align_bytes=64)
+        w_codes = keep.tile([P, PASSES, N], U32, align_bytes=64)
+        w_scales = keep.tile([P, PASSES, N], U8, align_bytes=64)
+        for g in range(PASSES):
+            side_by_side(nc.scalar.copy, w_grouped[:, g], w_planes[:, g])
+
+        def quantise_weights():
+            nc.vector.quantize_mx(
+                out=w_codes[:].rearrange("p g n -> p (g n)").bitcast(FP8X4),
+                scales=w_scales[:].rearrange("p g n -> p (g n)"),
+                in_=w_grouped[:].rearrange("p g n t -> p (g n t)"),
+            )
+
+        mean_var = {}
+        normed = {}
+        grouped_of = {}
+        codes_of = {}
+        sums_of = {}
+
+        def statistics(u):
+            parts = stat.tile([P, UNIT_TILES, BN_PARTS, 6], F32)
+            mv = stat.tile([P, UNIT_TILES, 2], F32)
+            for j in range(UNIT_TILES):
+                for b in range(BN_PARTS):
+                    nc.vector.bn_stats(
+                        out=parts[:, j, b, :], in_=x[u][:, j, b * BN_WIDTH : (b + 1) * BN_WIDTH]
+                    )
+                nc.vector.bn_aggr(out=mv[:, j, :], in_=parts[:, j].rearrange("p b s -> p (b s)"))
+            mean_var[u] = mv
+
+        def normalise(u):
+            mv = mean_var[u]
+            var_eps = stat.tile([P, UNIT_TILES], F32)
+            rstd = stat.tile([P, UNIT_TILES], F32)
+            neg_mean = stat.tile([P, UNIT_TILES], F32)
+            nc.gpsimd.tensor_scalar(
+                out=var_eps[:], in0=mv[:, :, 1], scalar1=1.0, scalar2=EPS, op0=ALU.mult, op1=ALU.add
+            )
+            nc.gpsimd.tensor_tensor(out=rstd[:], in0=var_eps[:], in1=minus_half[:], op=ALU.pow)
+            nc.gpsimd.tensor_scalar(
+                out=neg_mean[:], in0=mv[:, :, 0], scalar1=-1.0, scalar2=0.0, op0=ALU.mult, op1=ALU.add
+            )
+            y = work.tile([P, UNIT_TILES, D], F32)
+            for j in range(UNIT_TILES):
+                nc.gpsimd.tensor_scalar(
+                    out=y[:, j, :],
+                    in0=x[u][:, j, :],
+                    scalar1=neg_mean[:, j : j + 1],
+                    scalar2=rstd[:, j : j + 1],
+                    op0=ALU.add,
+                    op1=ALU.mult,
+                )
+            normed[u] = y
+
+        def turn_and_scale(u):
+            y = normed[u]
+            planes = work.tile([P, CHUNKS, UNIT_COLS], BF16)
+            for first in range(0, CHUNKS, BANK_CHUNKS):
+                turned = turned_pool.tile([P, BANK_CHUNKS, UNIT_COLS], F32, tag="turned")
+                for b in range(BANK_CHUNKS):
+                    c = first + b
+                    for j in range(UNIT_TILES):
+                        nc.tensor.transpose(
+                            turned[:, b, j * P : (j + 1) * P], y[:, j, c * P : (c + 1) * P], ident[:]
+                        )
+                for b in range(BANK_CHUNKS):
+                    c = first + b
+                    nc.scalar.activation(
+                        out=planes[:, c, :],
+                        in_=turned[:, b, :],
+                        func=ACT.Identity,
+                        scale=gain_shift[:, c : c + 1],
+                        bias=gain_shift[:, CHUNKS + c : CHUNKS + c + 1],
+                    )
+            grouped = work.tile([P, PASSES, UNIT_COLS, PACK], BF16, align_bytes=64)
+            for g in range(PASSES):
+                side_by_side(nc.scalar.copy, grouped[:, g], planes[:, g * PACK : (g + 1) * PACK, :])
+            grouped_of[u] = grouped
+
+        def quantise(u):
+            codes = work.tile([P, PASSES, UNIT_COLS], U32, align_bytes=64)
+            scales = work.tile([P, PASSES, UNIT_COLS], U8, align_bytes=64)
+            nc.vector.quantize_mx(
+                out=codes[:].rearrange("p g c -> p (g c)").bitcast(FP8X4),
+                scales=scales[:].rearrange("p g c -> p (g c)"),
+                in_=grouped_of[u][:].rearrange("p g c t -> p (g c t)"),
+            )
+            codes_of[u] = (codes, scales)
+
+        def project(u):
+            codes, scales = codes_of[u]
+            sums_of[u] = []
+            for j in range(UNIT_TILES):
+                rows = slice(j * P, (j + 1) * P)
+                sums = sums_pool.tile([P, N], F32)
+                for g in range(PASSES):
+                    nc.tensor.matmul_mx(
+                        out=sums[:],
+                        lhsT=codes[:, g, rows].bitcast(FP8X4),
+                        lhsT_scale=scales[:, g, rows],
+                        rhs=w_codes[:, g, :].bitcast(FP8X4),
+                        rhs_scale=w_scales[:, g, :],
+                        start=(g == 0),
+                        stop=(g == PASSES - 1),
+                    )
+                sums_of[u].append(sums)
+
+        def finish(u):
+            result = work.tile([P, UNIT_TILES, N], F32)
+            for j in range(UNIT_TILES):
+                nc.vector.tensor_tensor(
+                    out=result[:, j, :], in0=sums_of[u][j][:], in1=bias[:], op=ALU.add
+                )
+            nc.sync.dma_start(out=out_units[u], in_=result[:])
+
+        for step in range(UNITS + 4):
+            if step < UNITS:
+                statistics(step)
+            if step == 2:
+                quantise_weights()
+            if 0 <= step - 1 < UNITS:
+                normalise(step - 1)
+            if 0 <= step - 2 < UNITS:
+                turn_and_scale(step - 2)
+            if 0 <= step - 3 < UNITS:
+                quantise(step - 3)
+                project(step - 3)
+            if 0 <= step - 4 < UNITS:
+                finish(step - 4)

@@ -114,22 +114,18 @@ def tile_stulayer_pa_t_kernel(tc, src, ln1_w, ln1_b, w_uvqk, b_uvqk, out):
             mv = mean_var[u]
             var_eps = stat.tile([P, UNIT_TILES], F32)
             rstd = stat.tile([P, UNIT_TILES], F32)
-            neg_mean = stat.tile([P, UNIT_TILES], F32)
             nc.gpsimd.tensor_scalar(
                 out=var_eps[:], in0=mv[:, :, 1], scalar1=1.0, scalar2=EPS, op0=ALU.mult, op1=ALU.add
             )
             nc.gpsimd.tensor_tensor(out=rstd[:], in0=var_eps[:], in1=minus_half[:], op=ALU.pow)
-            nc.gpsimd.tensor_scalar(
-                out=neg_mean[:], in0=mv[:, :, 0], scalar1=-1.0, scalar2=0.0, op0=ALU.mult, op1=ALU.add
-            )
             y = work.tile([P, UNIT_TILES, D], F32)
             for j in range(UNIT_TILES):
-                nc.gpsimd.tensor_scalar(
+                nc.vector.tensor_scalar(
                     out=y[:, j, :],
                     in0=x[u][:, j, :],
-                    scalar1=neg_mean[:, j : j + 1],
+                    scalar1=mv[:, j, 0:1],
                     scalar2=rstd[:, j : j + 1],
-                    op0=ALU.add,
+                    op0=ALU.subtract,
                     op1=ALU.mult,
                 )
             normed[u] = y

@@ -25,6 +25,7 @@ UNIT_COLS = UNIT_TILES * P
 UNITS = ROWS // UNIT_COLS
 BANK_F32 = 512
 BANK_CHUNKS = BANK_F32 // UNIT_COLS
+PIPELINE_DEPTH = 4
 
 FLOPS = 2 * ROWS * D * N
 
@@ -47,6 +48,7 @@ def tile_stulayer_pa_t_kernel(tc, src, ln1_w, ln1_b, w_uvqk, b_uvqk, out):
         tc.tile_pool(name="work", bufs=3) as work,
         tc.psum_pool(name="turned", bufs=4) as turned_pool,
         tc.psum_pool(name="sums", bufs=4) as sums_pool,
+        tc.manual_schedule(),
     ):
         x = []
         for u in range(UNITS):
@@ -56,8 +58,11 @@ def tile_stulayer_pa_t_kernel(tc, src, ln1_w, ln1_b, w_uvqk, b_uvqk, out):
         nc.sync.dma_start(
             out=w_planes[:], in_=w_uvqk.rearrange("(g t p) n -> p g t n", t=PACK, p=P)
         )
+        bias = keep.tile([P, N], BF16)
         for u in range(1, UNITS):
             nc.sync.dma_start(out=x[u][:], in_=src_units[u])
+            if u == PIPELINE_DEPTH:
+                nc.sync.dma_start(out=bias[:], in_=b_uvqk.partition_broadcast(P))
 
         vec_rows = keep.tile([P, P], BF16)
         nc.vector.memset(vec_rows[:], 0.0)
@@ -65,8 +70,6 @@ def tile_stulayer_pa_t_kernel(tc, src, ln1_w, ln1_b, w_uvqk, b_uvqk, out):
         nc.scalar.dma_start(
             out=vec_rows[CHUNKS : 2 * CHUNKS, :], in_=ln1_b.rearrange("(c p) -> c p", p=P)
         )
-        bias = keep.tile([P, N], BF16)
-        nc.scalar.dma_start(out=bias[:], in_=b_uvqk.partition_broadcast(P))
 
         ident = keep.tile([P, P], F32)
         make_identity(nc, ident[:])
@@ -74,11 +77,11 @@ def tile_stulayer_pa_t_kernel(tc, src, ln1_w, ln1_b, w_uvqk, b_uvqk, out):
         nc.vector.memset(minus_half[:], -0.5)
 
         vec_f32 = keep.tile([P, P], F32)
-        nc.vector.tensor_copy(out=vec_f32[:], in_=vec_rows[:])
+        nc.scalar.copy(out=vec_f32[:], in_=vec_rows[:])
         vec_turned = turned_pool.tile([P, BANK_CHUNKS, UNIT_COLS], F32, tag="turned")
         nc.tensor.transpose(vec_turned[:, 0, 0:P], vec_f32[:], ident[:])
         gain_shift = keep.tile([P, 2 * CHUNKS], F32)
-        nc.vector.tensor_copy(out=gain_shift[:], in_=vec_turned[:, 0, 0 : 2 * CHUNKS])
+        nc.scalar.copy(out=gain_shift[:], in_=vec_turned[:, 0, 0 : 2 * CHUNKS])
 
         w_grouped = keep.tile([P, PASSES, N, PACK], BF16, align_bytes=64)
         w_codes = keep.tile([P, PASSES, N], U32, align_bytes=64)
@@ -114,18 +117,22 @@ def tile_stulayer_pa_t_kernel(tc, src, ln1_w, ln1_b, w_uvqk, b_uvqk, out):
             mv = mean_var[u]
             var_eps = stat.tile([P, UNIT_TILES], F32)
             rstd = stat.tile([P, UNIT_TILES], F32)
+            neg_mean = stat.tile([P, UNIT_TILES], F32)
             nc.gpsimd.tensor_scalar(
                 out=var_eps[:], in0=mv[:, :, 1], scalar1=1.0, scalar2=EPS, op0=ALU.mult, op1=ALU.add
             )
             nc.gpsimd.tensor_tensor(out=rstd[:], in0=var_eps[:], in1=minus_half[:], op=ALU.pow)
+            nc.gpsimd.tensor_scalar(
+                out=neg_mean[:], in0=mv[:, :, 0], scalar1=-1.0, scalar2=0.0, op0=ALU.mult, op1=ALU.add
+            )
             y = work.tile([P, UNIT_TILES, D], F32)
             for j in range(UNIT_TILES):
-                nc.vector.tensor_scalar(
+                nc.gpsimd.tensor_scalar(
                     out=y[:, j, :],
                     in0=x[u][:, j, :],
-                    scalar1=mv[:, j, 0:1],
+                    scalar1=neg_mean[:, j : j + 1],
                     scalar2=rstd[:, j : j + 1],
-                    op0=ALU.subtract,
+                    op0=ALU.add,
                     op1=ALU.mult,
                 )
             normed[u] = y
@@ -191,7 +198,7 @@ def tile_stulayer_pa_t_kernel(tc, src, ln1_w, ln1_b, w_uvqk, b_uvqk, out):
                 )
             nc.sync.dma_start(out=out_units[u], in_=result[:])
 
-        for step in range(UNITS + 4):
+        for step in range(UNITS + PIPELINE_DEPTH):
             if step < UNITS:
                 statistics(step)
             if step == 2:
@@ -203,5 +210,5 @@ def tile_stulayer_pa_t_kernel(tc, src, ln1_w, ln1_b, w_uvqk, b_uvqk, out):
             if 0 <= step - 3 < UNITS:
                 quantise(step - 3)
                 project(step - 3)
-            if 0 <= step - 4 < UNITS:
-                finish(step - 4)
+            if 0 <= step - PIPELINE_DEPTH < UNITS:
+                finish(step - PIPELINE_DEPTH)

@@ -86,10 +86,10 @@ def tile_stulayer_pa_t_kernel(tc, src, ln1_w, ln1_b, w_uvqk, b_uvqk, out):
         w_grouped = keep.tile([P, PASSES, N, PACK], BF16, align_bytes=64)
         w_codes = keep.tile([P, PASSES, N], U32, align_bytes=64)
         w_scales = keep.tile([P, PASSES, N], U8, align_bytes=64)
-        for g in range(PASSES):
-            side_by_side(nc.scalar.copy, w_grouped[:, g], w_planes[:, g])
 
         def quantise_weights():
+            for g in range(PASSES):
+                side_by_side(nc.vector.tensor_copy, w_grouped[:, g], w_planes[:, g])
             nc.vector.quantize_mx(
                 out=w_codes[:].rearrange("p g n -> p (g n)").bitcast(FP8X4),
                 scales=w_scales[:].rearrange("p g n -> p (g n)"),
@@ -159,7 +159,18 @@ def tile_stulayer_pa_t_kernel(tc, src, ln1_w, ln1_b, w_uvqk, b_uvqk, out):
                     )
             grouped = work.tile([P, PASSES, UNIT_COLS, PACK], BF16, align_bytes=64)
             for g in range(PASSES):
-                side_by_side(nc.scalar.copy, grouped[:, g], planes[:, g * PACK : (g + 1) * PACK, :])
+                pass_planes = planes[:, g * PACK : (g + 1) * PACK, :]
+                if g == PASSES - 1 and u % 2 == 1:
+                    nc.gpsimd.tensor_scalar(
+                        out=grouped[:, g],
+                        in0=pass_planes.rearrange("p t c -> p c t"),
+                        scalar1=1.0,
+                        scalar2=0.0,
+                        op0=ALU.mult,
+                        op1=ALU.add,
+                    )
+                else:
+                    side_by_side(nc.scalar.copy, grouped[:, g], pass_planes)
             grouped_of[u] = grouped
 
         def quantise(u):

@@ -86,10 +86,10 @@ def tile_stulayer_pa_t_kernel(tc, src, ln1_w, ln1_b, w_uvqk, b_uvqk, out):
         w_grouped = keep.tile([P, PASSES, N, PACK], BF16, align_bytes=64)
         w_codes = keep.tile([P, PASSES, N], U32, align_bytes=64)
         w_scales = keep.tile([P, PASSES, N], U8, align_bytes=64)
+        for g in range(PASSES):
+            side_by_side(nc.scalar.copy, w_grouped[:, g], w_planes[:, g])
 
         def quantise_weights():
-            for g in range(PASSES):
-                side_by_side(nc.vector.tensor_copy, w_grouped[:, g], w_planes[:, g])
             nc.vector.quantize_mx(
                 out=w_codes[:].rearrange("p g n -> p (g n)").bitcast(FP8X4),
                 scales=w_scales[:].rearrange("p g n -> p (g n)"),
@@ -98,6 +98,7 @@ def tile_stulayer_pa_t_kernel(tc, src, ln1_w, ln1_b, w_uvqk, b_uvqk, out):
 
         mean_var = {}
         normed = {}
+        planes_of = {}
         grouped_of = {}
         codes_of = {}
         sums_of = {}
@@ -158,20 +159,23 @@ def tile_stulayer_pa_t_kernel(tc, src, ln1_w, ln1_b, w_uvqk, b_uvqk, out):
                         bias=gain_shift[:, CHUNKS + c : CHUNKS + c + 1],
                     )
             grouped = work.tile([P, PASSES, UNIT_COLS, PACK], BF16, align_bytes=64)
-            for g in range(PASSES):
-                pass_planes = planes[:, g * PACK : (g + 1) * PACK, :]
-                if g == PASSES - 1 and u % 2 == 1:
-                    nc.gpsimd.tensor_scalar(
-                        out=grouped[:, g],
-                        in0=pass_planes.rearrange("p t c -> p c t"),
-                        scalar1=1.0,
-                        scalar2=0.0,
-                        op0=ALU.mult,
-                        op1=ALU.add,
-                    )
-                else:
-                    side_by_side(nc.scalar.copy, grouped[:, g], pass_planes)
+            planes_of[u] = planes
             grouped_of[u] = grouped
+            for g in range(PASSES):
+                if not vector_regroups(u, g):
+                    side_by_side(nc.scalar.copy, grouped[:, g], planes[:, g * PACK : (g + 1) * PACK, :])
+
+        def vector_regroups(u, g):
+            return g == PASSES - 1 and u % 2 == 1
+
+        def regroup_on_vector(u):
+            for g in range(PASSES):
+                if vector_regroups(u, g):
+                    side_by_side(
+                        nc.vector.tensor_copy,
+                        grouped_of[u][:, g],
+                        planes_of[u][:, g * PACK : (g + 1) * PACK, :],
+                    )
 
         def quantise(u):
             codes = work.tile([P, PASSES, UNIT_COLS], U32, align_bytes=64)
@@ -223,3 +227,5 @@ def tile_stulayer_pa_t_kernel(tc, src, ln1_w, ln1_b, w_uvqk, b_uvqk, out):
                 project(step - 3)
             if 0 <= step - PIPELINE_DEPTH < UNITS:
                 finish(step - PIPELINE_DEPTH)
+            if 0 <= step - 2 < UNITS:
+                regroup_on_vector(step - 2)

import concourse.mybir as mybir
from concourse.masks import make_identity

F32 = mybir.dt.float32
BF16 = mybir.dt.bfloat16
U32 = mybir.dt.uint32
U8 = mybir.dt.uint8
FP8X4 = mybir.dt.float8_e4m3fn_x4
ALU = mybir.AluOpType
ACT = mybir.ActivationFunctionType

P = 128
ROWS = 2048 * 2
D = 1024
N = 512
EPS = 1e-5
PACK = 4
K_PASS = P * PACK
PASSES = D // K_PASS
CHUNKS = D // P
BN_WIDTH = 512
BN_PARTS = D // BN_WIDTH
UNIT_TILES = 2
UNIT_COLS = UNIT_TILES * P
UNITS = ROWS // UNIT_COLS
BANK_F32 = 512
BANK_CHUNKS = BANK_F32 // UNIT_COLS
PIPELINE_DEPTH = 4

FLOPS = 2 * ROWS * D * N


def side_by_side(copy, grouped, planes):
    copy(
        out=grouped.rearrange("p (c i) t -> p c t i", i=4),
        in_=planes.rearrange("p t (c i) -> p c t i", i=4),
    )


def tile_stulayer_pa_t_kernel(tc, src, ln1_w, ln1_b, w_uvqk, b_uvqk, out):
    nc = tc.nc
    src_units = src.flatten_outer_dims().rearrange("(u p j) d -> u p j d", p=P, j=UNIT_TILES)
    out_units = out.flatten_outer_dims().rearrange("(u p j) n -> u p j n", p=P, j=UNIT_TILES)

    with (
        tc.tile_pool(name="keep", bufs=1) as keep,
        tc.tile_pool(name="stat", bufs=4) as stat,
        tc.tile_pool(name="work", bufs=3) as work,
        tc.psum_pool(name="turned", bufs=4) as turned_pool,
        tc.psum_pool(name="sums", bufs=4) as sums_pool,
        tc.manual_schedule(),
    ):
        x = []
        for u in range(UNITS):
            x.append(keep.tile([P, UNIT_TILES, D], BF16, name="x%d" % u))
        w_planes = keep.tile([P, PASSES, PACK, N], BF16)
        nc.sync.dma_start(out=x[0][:], in_=src_units[0])
        nc.sync.dma_start(
            out=w_planes[:], in_=w_uvqk.rearrange("(g t p) n -> p g t n", t=PACK, p=P)
        )
        bias = keep.tile([P, N], BF16)
        for u in range(1, UNITS):
            nc.sync.dma_start(out=x[u][:], in_=src_units[u])
            if u == PIPELINE_DEPTH:
                nc.sync.dma_start(out=bias[:], in_=b_uvqk.partition_broadcast(P))

        vec_rows = keep.tile([P, P], BF16)
        nc.vector.memset(vec_rows[:], 0.0)
        nc.scalar.dma_start(out=vec_rows[0:CHUNKS, :], in_=ln1_w.rearrange("(c p) -> c p", p=P))
        nc.scalar.dma_start(
            out=vec_rows[CHUNKS : 2 * CHUNKS, :], in_=ln1_b.rearrange("(c p) -> c p", p=P)
        )

        ident = keep.tile([P, P], F32)
        make_identity(nc, ident[:])
        minus_half = keep.tile([P, UNIT_TILES], F32)
        nc.vector.memset(minus_half[:], -0.5)

        vec_f32 = keep.tile([P, P], F32)
        nc.scalar.copy(out=vec_f32[:], in_=vec_rows[:])
        vec_turned = turned_pool.tile([P, BANK_CHUNKS, UNIT_COLS], F32, tag="turned")
        nc.tensor.transpose(vec_turned[:, 0, 0:P], vec_f32[:], ident[:])
        gain_shift = keep.tile([P, 2 * CHUNKS], F32)
        nc.scalar.copy(out=gain_shift[:], in_=vec_turned[:, 0, 0 : 2 * CHUNKS])

        w_grouped = keep.tile([P, PASSES, N, PACK], BF16, align_bytes=64)
        w_codes = keep.tile([P, PASSES, N], U32, align_bytes=64)
        w_scales = keep.tile([P, PASSES, N], U8, align_bytes=64)
        for g in range(PASSES):
            side_by_side(nc.scalar.copy, w_grouped[:, g], w_planes[:, g])

        def quantise_weights():
            nc.vector.quantize_mx(
                out=w_codes[:].rearrange("p g n -> p (g n)").bitcast(FP8X4),
                scales=w_scales[:].rearrange("p g n -> p (g n)"),
                in_=w_grouped[:].rearrange("p g n t -> p (g n t)"),
            )

        mean_var = {}
        normed = {}
        planes_of = {}
        grouped_of = {}
        codes_of = {}
        sums_of = {}

        def statistics(u):
            parts = stat.tile([P, UNIT_TILES, BN_PARTS, 6], F32)
            mv = stat.tile([P, UNIT_TILES, 2], F32)
            for j in range(UNIT_TILES):
                for b in range(BN_PARTS):
                    nc.vector.bn_stats(
                        out=parts[:, j, b, :], in_=x[u][:, j, b * BN_WIDTH : (b + 1) * BN_WIDTH]
                    )
                nc.vector.bn_aggr(out=mv[:, j, :], in_=parts[:, j].rearrange("p b s -> p (b s)"))
            mean_var[u] = mv

        def normalise(u):
            mv = mean_var[u]
            var_eps = stat.tile([P, UNIT_TILES], F32)
            rstd = stat.tile([P, UNIT_TILES], F32)
            neg_mean = stat.tile([P, UNIT_TILES], F32)
            nc.gpsimd.tensor_scalar(
                out=var_eps[:], in0=mv[:, :, 1], scalar1=1.0, scalar2=EPS, op0=ALU.mult, op1=ALU.add
            )
            nc.gpsimd.tensor_tensor(out=rstd[:], in0=var_eps[:], in1=minus_half[:], op=ALU.pow)
            nc.gpsimd.tensor_scalar(
                out=neg_mean[:], in0=mv[:, :, 0], scalar1=-1.0, scalar2=0.0, op0=ALU.mult, op1=ALU.add
            )
            y = work.tile([P, UNIT_TILES, D], F32)
            for j in range(UNIT_TILES):
                nc.gpsimd.tensor_scalar(
                    out=y[:, j, :],
                    in0=x[u][:, j, :],
                    scalar1=neg_mean[:, j : j + 1],
                    scalar2=rstd[:, j : j + 1],
                    op0=ALU.add,
                    op1=ALU.mult,
                )
            normed[u] = y

        def turn_and_scale(u):
            y = normed[u]
            planes = work.tile([P, CHUNKS, UNIT_COLS], BF16)
            for first in range(0, CHUNKS, BANK_CHUNKS):
                turned = turned_pool.tile([P, BANK_CHUNKS, UNIT_COLS], F32, tag="turned")
                for b in range(BANK_CHUNKS):
                    c = first + b
                    for j in range(UNIT_TILES):
                        nc.tensor.transpose(
                            turned[:, b, j * P : (j + 1) * P], y[:, j, c * P : (c + 1) * P], ident[:]
                        )
                for b in range(BANK_CHUNKS):
                    c = first + b
                    nc.scalar.activation(
                        out=planes[:, c, :],
                        in_=turned[:, b, :],
                        func=ACT.Identity,
                        scale=gain_shift[:, c : c + 1],
                        bias=gain_shift[:, CHUNKS + c : CHUNKS + c + 1],
                    )
            grouped = work.tile([P, PASSES, UNIT_COLS, PACK], BF16, align_bytes=64)
            planes_of[u] = planes
            grouped_of[u] = grouped
            for g in range(PASSES):
                if not vector_regroups(u, g):
                    side_by_side(nc.scalar.copy, grouped[:, g], planes[:, g * PACK : (g + 1) * PACK, :])

        def vector_regroups(u, g):
            return g == PASSES - 1 and u % 2 == 1

        def regroup_on_vector(u):
            for g in range(PASSES):
                if vector_regroups(u, g):
                    side_by_side(
                        nc.vector.tensor_copy,
                        grouped_of[u][:, g],
                        planes_of[u][:, g * PACK : (g + 1) * PACK, :],
                    )

        def quantise(u):
            codes = work.tile([P, PASSES, UNIT_COLS], U32, align_bytes=64)
            scales = work.tile([P, PASSES, UNIT_COLS], U8, align_bytes=64)
            nc.vector.quantize_mx(
                out=codes[:].rearrange("p g c -> p (g c)").bitcast(FP8X4),
                scales=scales[:].rearrange("p g c -> p (g c)"),
                in_=grouped_of[u][:].rearrange("p g c t -> p (g c t)"),
            )
            codes_of[u] = (codes, scales)

        def project(u):
            codes, scales = codes_of[u]
            sums_of[u] = []
            for j in range(UNIT_TILES):
                rows = slice(j * P, (j + 1) * P)
                sums = sums_pool.tile([P, N], F32)
                for g in range(PASSES):
                    nc.tensor.matmul_mx(
                        out=sums[:],
                        lhsT=codes[:, g, rows].bitcast(FP8X4),
                        lhsT_scale=scales[:, g, rows],
                        rhs=w_codes[:, g, :].bitcast(FP8X4),
                        rhs_scale=w_scales[:, g, :],
                        start=(g == 0),
                        stop=(g == PASSES - 1),
                    )
                sums_of[u].append(sums)

        def finish(u):
            result = work.tile([P, UNIT_TILES, N], F32)
            for j in range(UNIT_TILES):
                nc.vector.tensor_tensor(
                    out=result[:, j, :], in0=sums_of[u][j][:], in1=bias[:], op=ALU.add
                )
            nc.sync.dma_start(out=out_units[u], in_=result[:])

        for step in range(UNITS + PIPELINE_DEPTH):
            if step < UNITS:
                statistics(step)
            if step == 2:
                quantise_weights()
            if 0 <= step - 1 < UNITS:
                normalise(step - 1)
            if 0 <= step - 2 < UNITS:
                turn_and_scale(step - 2)
            if 0 <= step - 3 < UNITS:
                quantise(step - 3)
                project(step - 3)
            if 0 <= step - PIPELINE_DEPTH < UNITS:
                finish(step - PIPELINE_DEPTH)
            if 0 <= step - 2 < UNITS:
                regroup_on_vector(step - 2)
